import numpy as np
import ml_dtypes


def mxq(x, axis, fmt="e4m3"):
    dtype, down = {"e4m3": (ml_dtypes.float8_e4m3fn, 7), "e5m2": (ml_dtypes.float8_e5m2, 14)}[fmt]
    v = np.moveaxis(np.asarray(x, np.float32).astype(ml_dtypes.bfloat16).astype(np.float64), axis, -1)
    blocks = v.reshape(v.shape[:-1] + (-1, 32))
    amax = np.abs(blocks).max(-1, keepdims=True)
    byte = np.maximum(np.where(amax > 0, np.frexp(amax)[1] - 1 + 127, 0) - down, 1)
    scale = np.exp2(byte - 127.0)
    codes = (blocks / scale).astype(np.float32).astype(dtype).astype(np.float64)
    return np.moveaxis((codes * scale).reshape(v.shape), -1, axis)


WIDE = False


def mx_kscale(k):
    if not WIDE:
        return np.ones(k)
    levels = np.array([10, -10, 5, -5, 0])
    a = np.random.permutation(np.resize(levels, k // 512 * 4)).reshape(k // 512, 4)
    idx = np.arange(k)
    return np.exp2(a[idx // 512, idx % 128 // 32])


BF16 = ml_dtypes.bfloat16


def bf(x):
    return np.asarray(x, np.float32).astype(BF16)


def f64(x):
    return np.asarray(x).astype(np.float64)


B, S, D, DFF, R = 4, 2048, 1024, 512, 512


def erf(z):
    z2 = z * z
    acc = np.zeros_like(z)
    for c in (np.arange(13) + 0.5) ** 2 * 0.25:
        acc += np.exp(-c) / (c + z2)
    return np.tanh(2.0 * np.pi * z) - z * np.exp(-z2) / np.pi * acc


def gelu_erf(v):
    return 0.5 * v * (1.0 + erf(v / np.sqrt(2.0)))


def setup_inputs():
    s, r = mx_kscale(D), mx_kscale(R)
    return {"x": bf(np.random.standard_normal((B, S, D)) * s),
            "c_fc_U": bf(np.random.standard_normal((D, R)) * 2.0 / np.sqrt(D) / s[:, None]),
            "c_fc_S": bf(np.random.uniform(size=R) * r),
            "c_fc_V": bf(np.random.standard_normal((DFF, R)) / np.sqrt(R) / r[None, :]),
            "c_fc_bias": bf(np.random.standard_normal(DFF) * 0.3)}


def reference(x, c_fc_U, c_fc_S, c_fc_V, c_fc_bias):
    us = f64(c_fc_U) * f64(c_fc_S)[None, :]
    w = mxq(us, 1, "e4m3") @ mxq(f64(c_fc_V), 1, "e4m3").T
    h = (mxq(f64(x), 2, "e4m3") @ mxq(w, 0, "e4m3")) + f64(c_fc_bias)
    return gelu_erf(h)

@@ -1,0 +1,235 @@
+from contextlib import ExitStack
+
+import concourse.mybir as mybir
+from concourse.masks import make_identity
+
+F32 = mybir.dt.float32
+BF16 = mybir.dt.bfloat16
+U32 = mybir.dt.uint32
+U8 = mybir.dt.uint8
+FP8X4 = mybir.dt.float8_e4m3fn_x4
+GELU = mybir.ActivationFunctionType.Gelu
+MULT = mybir.AluOpType.mult
+ADD = mybir.AluOpType.add
+
+P = 128
+TOKENS = 8192
+D = 1024
+DFF = 512
+RANK = 512
+FLOPS = 2 * D * RANK * DFF + 2 * TOKENS * D * DFF
+
+J = 4
+NG = TOKENS // (P * J)
+XBUFS = 8
+PIN = False
+
+
+def tile_hybridsuperlayer_pa_t_kernel(tc, x, c_fc_U, c_fc_S, c_fc_V, c_fc_bias, out):
+    nc = tc.nc
+    x_groups = x.flatten_outer_dims().rearrange("(n p j) k -> n p (j k)", p=P, j=J)
+    out_groups = out.flatten_outer_dims().rearrange("(n p j) f -> n p (j f)", p=P, j=J)
+
+    with ExitStack() as ctx:
+        if PIN:
+            ctx.enter_context(tc.manual_schedule())
+        keep = ctx.enter_context(tc.tile_pool(name="keep", bufs=1))
+        xin = ctx.enter_context(tc.tile_pool(name="xin", bufs=XBUFS))
+        xgr = ctx.enter_context(tc.tile_pool(name="xgr", bufs=3))
+        xq = ctx.enter_context(tc.tile_pool(name="xq", bufs=4))
+        res = ctx.enter_context(tc.tile_pool(name="res", bufs=6))
+        ps_t = ctx.enter_context(tc.psum_pool(name="ps_t", bufs=4))
+        ps_a = ctx.enter_context(tc.psum_pool(name="ps_a", bufs=4))
+
+        s_rows = keep.tile([P, 256], BF16, name="s_rows")
+        b_rows = keep.tile([P, DFF], BF16, name="b_rows")
+        ones = keep.tile([P, P], BF16, name="ones")
+        warm = keep.tile([P, 8], F32, name="warm")
+        ident = keep.tile([P, P], F32, name="ident")
+        nc.vector.memset(s_rows[:], 0.0)
+        nc.vector.memset(b_rows[:], 0.0)
+        nc.vector.memset(ones[:], 1.0)
+        nc.vector.memset(warm[:], 0.0)
+        make_identity(nc, ident[:])
+
+        u_sb = keep.tile([P, 4, 2 * RANK], BF16, name="u_sb")
+        v_sb = keep.tile([P, 4, RANK], BF16, name="v_sb")
+        u_view = c_fc_U.rearrange("(c p e) r -> p c (e r)", c=4, p=P, e=2)
+        nc.sync.dma_start(out=s_rows[0:2, :], in_=c_fc_S.rearrange("(u w) -> u w", u=2))
+        nc.sync.dma_start(out=u_sb[:, 0:2, :], in_=u_view[:, 0:2, :])
+        nc.sync.dma_start(out=v_sb[:], in_=c_fc_V.rearrange("(c p) r -> p c r", p=P))
+        nc.sync.dma_start(out=u_sb[:, 2:4, :], in_=u_view[:, 2:4, :])
+        nc.sync.dma_start(out=b_rows[0:1, :], in_=c_fc_bias.rearrange("(o f) -> o f", o=1))
+
+        x_tiles = {}
+
+        def load(n):
+            x_sb = xin.tile([P, J * D], BF16, name="x_sb", tag="x_sb")
+            nc.sync.dma_start(out=x_sb[:], in_=x_groups[n])
+            x_tiles[n] = x_sb
+
+        for n in range(XBUFS):
+            load(n)
+
+        nc.scalar.activation(out=warm[:], in_=warm[:], func=GELU)
+
+        s_ps = ps_t.tile([P, 4, P], F32, name="s_ps", tag="t")
+        nc.tensor.transpose(s_ps[:, 0, :], s_rows[:].bitcast(F32), ident[:])
+        s_col = keep.tile([P, 4], BF16, name="s_col")
+        nc.vector.tensor_copy(out=s_col[:], in_=s_ps[:, 0, 0:2].bitcast(BF16))
+
+        u_words = u_sb[:].bitcast(F32)
+        v_words = v_sb[:].bitcast(F32)
+        g_u = keep.tile([P, 8 * 512], BF16, name="g_u", align_bytes=64)
+        g_v = keep.tile([P, 4 * 512], BF16, name="g_v", align_bytes=64)
+        g_u_words = g_u[:].bitcast(F32).rearrange("p (m d u) -> p m d u", m=8, d=P, u=2)
+        g_v_words = g_v[:].bitcast(F32).rearrange("p (c f u) -> p c f u", c=4, f=P, u=2)
+        u_codes = keep.tile([P, 8 * P], U32, name="u_codes", align_bytes=64)
+        u_scales = keep.tile([P, 8 * P], U8, name="u_scales", align_bytes=64)
+        v_codes = keep.tile([P, DFF], U32, name="v_codes", align_bytes=64)
+        v_scales = keep.tile([P, DFF], U8, name="v_scales", align_bytes=64)
+
+        def u_bank(b):
+            tp = ps_t.tile([P, 4, P], F32, name="tp_u", tag="t")
+            for mm in range(2):
+                m = 2 * b + mm
+                for u in range(2):
+                    lo = (m % 2) * 256 + u * P
+                    nc.tensor.transpose(tp[:, 2 * mm + u, :], u_words[:, m // 2, lo : lo + P], ident[:])
+            nc.scalar.copy(
+                out=g_u_words[:, 2 * b : 2 * b + 2],
+                in_=tp[:].rearrange("p (m u) d -> p m d u", u=2),
+            )
+
+        def u_half(g):
+            half = g_u[:, 2048 * g : 2048 * (g + 1)]
+            nc.vector.tensor_tensor(
+                out=half.rearrange("p (c t) -> p c t", t=4),
+                in0=half.rearrange("p (c t) -> p c t", t=4),
+                in1=s_col[:].unsqueeze(1).to_broadcast([P, 512, 4]),
+                op=MULT,
+            )
+            nc.vector.quantize_mx(
+                out=u_codes[:, 512 * g : 512 * (g + 1)].bitcast(FP8X4),
+                scales=u_scales[:, 512 * g : 512 * (g + 1)],
+                in_=half,
+            )
+
+        def v_bank(b):
+            tp = ps_t.tile([P, 4, P], F32, name="tp_v", tag="t")
+            for cc in range(2):
+                for u in range(2):
+                    nc.tensor.transpose(
+                        tp[:, 2 * cc + u, :], v_words[:, 2 * b + cc, u * P : (u + 1) * P], ident[:]
+                    )
+            nc.scalar.copy(
+                out=g_v_words[:, 2 * b : 2 * b + 2],
+                in_=tp[:].rearrange("p (c u) f -> p c f u", u=2),
+            )
+
+        u_bank(0)
+        u_bank(1)
+        v_bank(0)
+        v_bank(1)
+        u_half(0)
+        nc.vector.quantize_mx(out=v_codes[:].bitcast(FP8X4), scales=v_scales[:], in_=g_v[:])
+        u_bank(2)
+        u_bank(3)
+        u_half(1)
+
+        b_ps = ps_a.tile([P, DFF], F32, name="b_ps", tag="a")
+        nc.tensor.matmul(out=b_ps[:], lhsT=ones[:], rhs=b_rows[:], start=True, stop=True)
+        bias_bc = keep.tile([P, DFF], F32, name="bias_bc")
+        nc.scalar.copy(out=bias_bc[:], in_=b_ps[:])
+
+        grouped = {}
+        codes = {}
+
+        def flip(n):
+            words = x_tiles[n][:].bitcast(F32)
+            g_x = xgr.tile([P, J * D], BF16, name="g_x", tag="g_x", align_bytes=64)
+            g_x_words = g_x[:].bitcast(F32).rearrange("p (j g t u) -> p j g t u", j=J, g=2, t=P, u=2)
+            for j in range(J):
+                tp = ps_t.tile([P, 4, P], F32, name="tp_x", tag="t")
+                for q in range(4):
+                    lo = j * 512 + q * P
+                    nc.tensor.transpose(tp[:, q, :], words[:, lo : lo + P], ident[:])
+                src = tp[:].rearrange("p (g u) t -> p g t u", u=2)
+                if j == J - 1:
+                    nc.vector.tensor_copy(out=g_x_words[:, j], in_=src)
+                else:
+                    nc.scalar.copy(out=g_x_words[:, j], in_=src)
+            grouped[n] = g_x
+
+        def quantise(n):
+            x_codes = xq.tile([P, J * 256], U32, name="x_codes", tag="x_codes", align_bytes=64)
+            x_scales = xq.tile([P, J * 256], U8, name="x_scales", tag="x_scales", align_bytes=64)
+            nc.vector.quantize_mx(out=x_codes[:].bitcast(FP8X4), scales=x_scales[:], in_=grouped[n][:])
+            codes[n] = (x_codes, x_scales)
+
+        g_w = keep.tile([P, 2, DFF, 4], BF16, name="g_w", align_bytes=64)
+        w_codes = keep.tile([P, 2, DFF], U32, name="w_codes", align_bytes=64)
+        w_scales = keep.tile([P, 2, DFF], U8, name="w_scales", align_bytes=64)
+
+        def w_half(g):
+            for c in range(4):
+                wa = ps_a.tile([P, 4, P], F32, name="wa", tag="a")
+                for t in range(4):
+                    lo = (4 * g + t) * P
+                    nc.tensor.matmul_mx(
+                        out=wa[:, t, :],
+                        lhsT=u_codes[:, lo : lo + P].bitcast(FP8X4),
+                        lhsT_scale=u_scales[:, lo : lo + P],
+                        rhs=v_codes[:, c * P : (c + 1) * P].bitcast(FP8X4),
+                        rhs_scale=v_scales[:, c * P : (c + 1) * P],
+                        start=True,
+                        stop=True,
+                    )
+                dst = g_w[:, g, c * P : (c + 1) * P, :]
+                src = wa[:].rearrange("p t f -> p f t")
+                if c % 2 == 0:
+                    nc.scalar.copy(out=dst, in_=src)
+                else:
+                    nc.vector.tensor_copy(out=dst, in_=src)
+            nc.vector.quantize_mx(
+                out=w_codes[:, g, :].bitcast(FP8X4),
+                scales=w_scales[:, g, :],
+                in_=g_w[:, g].rearrange("p f t -> p (f t)"),
+            )
+
+        w_half(0)
+        flip(0)
+        w_half(1)
+        quantise(0)
+
+        def product(n, o_sb, j):
+            x_codes, x_scales = codes[n]
+            acc = ps_a.tile([P, DFF], F32, name="acc", tag="a")
+            for g in range(2):
+                lo = (2 * j + g) * P
+                nc.tensor.matmul_mx(
+                    out=acc[:],
+                    lhsT=x_codes[:, lo : lo + P].bitcast(FP8X4),
+                    lhsT_scale=x_scales[:, lo : lo + P],
+                    rhs=w_codes[:, g, :].bitcast(FP8X4),
+                    rhs_scale=w_scales[:, g, :],
+                    start=(g == 0),
+                    stop=(g == 1),
+                )
+            cols = o_sb[:, j * DFF : (j + 1) * DFF]
+            nc.vector.tensor_tensor(out=cols, in0=acc[:], in1=bias_bc[:], op=ADD)
+            nc.scalar.activation(out=cols, in_=cols, func=GELU)
+
+        for n in range(NG):
+            if n + 1 < NG:
+                flip(n + 1)
+            if n + XBUFS < NG:
+                load(n + XBUFS)
+            o_sb = res.tile([P, J * DFF], F32, name="o_sb", tag="o_sb")
+            product(n, o_sb, 0)
+            product(n, o_sb, 1)
+            if n + 1 < NG:
+                quantise(n + 1)
+            product(n, o_sb, 2)
+            product(n, o_sb, 3)
+            nc.sync.dma_start(out=out_groups[n], in_=o_sb[:])

@@ -22,7 +22,8 @@ FLOPS = 2 * D * RANK * DFF + 2 * TOKENS * D * DFF
 J = 4
 NG = TOKENS // (P * J)
 XBUFS = 8
-PIN = False
+PIN = True
+LAG = 2
 
 
 def tile_hybridsuperlayer_pa_t_kernel(tc, x, c_fc_U, c_fc_S, c_fc_V, c_fc_bias, out):
@@ -199,8 +200,11 @@ def tile_hybridsuperlayer_pa_t_kernel(tc, x, c_fc_U, c_fc_S, c_fc_V, c_fc_bias, 
 
         w_half(0)
         flip(0)
+        load(XBUFS)
         w_half(1)
         quantise(0)
+
+        waiting = []
 
         def product(n, o_sb, j):
             x_codes, x_scales = codes[n]
@@ -216,20 +220,31 @@ def tile_hybridsuperlayer_pa_t_kernel(tc, x, c_fc_U, c_fc_S, c_fc_V, c_fc_bias, 
                     start=(g == 0),
                     stop=(g == 1),
                 )
+            nc.vector.tensor_tensor(
+                out=o_sb[:, j * DFF : (j + 1) * DFF], in0=acc[:], in1=bias_bc[:], op=ADD
+            )
+            waiting.append((n, o_sb, j))
+
+        def finish(i):
+            n, o_sb, j = waiting[i]
             cols = o_sb[:, j * DFF : (j + 1) * DFF]
-            nc.vector.tensor_tensor(out=cols, in0=acc[:], in1=bias_bc[:], op=ADD)
             nc.scalar.activation(out=cols, in_=cols, func=GELU)
+            if n == NG - 1:
+                nc.sync.dma_start(out=out_groups[n][:, j * DFF : (j + 1) * DFF], in_=cols)
+            elif j == J - 1:
+                nc.sync.dma_start(out=out_groups[n], in_=o_sb[:])
 
         for n in range(NG):
             if n + 1 < NG:
                 flip(n + 1)
-            if n + XBUFS < NG:
-                load(n + XBUFS)
+            if n + 1 + XBUFS < NG:
+                load(n + 1 + XBUFS)
             o_sb = res.tile([P, J * DFF], F32, name="o_sb", tag="o_sb")
-            product(n, o_sb, 0)
-            product(n, o_sb, 1)
-            if n + 1 < NG:
-                quantise(n + 1)
-            product(n, o_sb, 2)
-            product(n, o_sb, 3)
-            nc.sync.dma_start(out=out_groups[n], in_=o_sb[:])
+            for j in range(J):
+                if j == 2 and n + 1 < NG:
+                    quantise(n + 1)
+                product(n, o_sb, j)
+                if n * J + j >= LAG:
+                    finish(n * J + j - LAG)
+        for i in range(NG * J - LAG, NG * J):
+            finish(i)

@@ -22,8 +22,9 @@ FLOPS = 2 * D * RANK * DFF + 2 * TOKENS * D * DFF
 J = 4
 NG = TOKENS // (P * J)
 XBUFS = 8
-PIN = True
 LAG = 2
+FINE_STORES = 3
+WARM = 0
 
 
 def tile_hybridsuperlayer_pa_t_kernel(tc, x, c_fc_U, c_fc_S, c_fc_V, c_fc_bias, out):
@@ -32,8 +33,7 @@ def tile_hybridsuperlayer_pa_t_kernel(tc, x, c_fc_U, c_fc_S, c_fc_V, c_fc_bias, 
     out_groups = out.flatten_outer_dims().rearrange("(n p j) f -> n p (j f)", p=P, j=J)
 
     with ExitStack() as ctx:
-        if PIN:
-            ctx.enter_context(tc.manual_schedule())
+        ctx.enter_context(tc.manual_schedule())
         keep = ctx.enter_context(tc.tile_pool(name="keep", bufs=1))
         xin = ctx.enter_context(tc.tile_pool(name="xin", bufs=XBUFS))
         xgr = ctx.enter_context(tc.tile_pool(name="xgr", bufs=3))
@@ -42,25 +42,19 @@ def tile_hybridsuperlayer_pa_t_kernel(tc, x, c_fc_U, c_fc_S, c_fc_V, c_fc_bias, 
         ps_t = ctx.enter_context(tc.psum_pool(name="ps_t", bufs=4))
         ps_a = ctx.enter_context(tc.psum_pool(name="ps_a", bufs=4))
 
-        s_rows = keep.tile([P, 256], BF16, name="s_rows")
-        b_rows = keep.tile([P, DFF], BF16, name="b_rows")
-        ones = keep.tile([P, P], BF16, name="ones")
-        warm = keep.tile([P, 8], F32, name="warm")
-        ident = keep.tile([P, P], F32, name="ident")
-        nc.vector.memset(s_rows[:], 0.0)
-        nc.vector.memset(b_rows[:], 0.0)
-        nc.vector.memset(ones[:], 1.0)
-        nc.vector.memset(warm[:], 0.0)
-        make_identity(nc, ident[:])
+        def copy_on(engine, dst, src):
+            if engine == "V":
+                nc.vector.tensor_copy(out=dst, in_=src)
+            else:
+                nc.scalar.copy(out=dst, in_=src)
 
         u_sb = keep.tile([P, 4, 2 * RANK], BF16, name="u_sb")
         v_sb = keep.tile([P, 4, RANK], BF16, name="v_sb")
         u_view = c_fc_U.rearrange("(c p e) r -> p c (e r)", c=4, p=P, e=2)
-        nc.sync.dma_start(out=s_rows[0:2, :], in_=c_fc_S.rearrange("(u w) -> u w", u=2))
-        nc.sync.dma_start(out=u_sb[:, 0:2, :], in_=u_view[:, 0:2, :])
+        nc.sync.dma_start(out=u_sb[:, 0:1, :], in_=u_view[:, 0:1, :])
+        nc.sync.dma_start(out=u_sb[:, 1:2, :], in_=u_view[:, 1:2, :])
         nc.sync.dma_start(out=v_sb[:], in_=c_fc_V.rearrange("(c p) r -> p c r", p=P))
         nc.sync.dma_start(out=u_sb[:, 2:4, :], in_=u_view[:, 2:4, :])
-        nc.sync.dma_start(out=b_rows[0:1, :], in_=c_fc_bias.rearrange("(o f) -> o f", o=1))
 
         x_tiles = {}
 
@@ -72,12 +66,19 @@ def tile_hybridsuperlayer_pa_t_kernel(tc, x, c_fc_U, c_fc_S, c_fc_V, c_fc_bias, 
         for n in range(XBUFS):
             load(n)
 
+        s_rows = keep.tile([P, 256], BF16, name="s_rows")
+        b_rows = keep.tile([P, DFF], BF16, name="b_rows")
+        ones = keep.tile([P, P], BF16, name="ones")
+        warm = keep.tile([P, 8], F32, name="warm")
+        ident = keep.tile([P, P], F32, name="ident")
+        nc.vector.memset(s_rows[:], 0.0)
+        nc.vector.memset(b_rows[:], 0.0)
+        nc.vector.memset(ones[:], 1.0)
+        nc.vector.memset(warm[:], 0.0)
+        make_identity(nc, ident[:])
+        nc.scalar.dma_start(out=s_rows[0:2, :], in_=c_fc_S.rearrange("(u w) -> u w", u=2))
+        nc.scalar.dma_start(out=b_rows[0:1, :], in_=c_fc_bias.rearrange("(o f) -> o f", o=1))
         nc.scalar.activation(out=warm[:], in_=warm[:], func=GELU)
-
-        s_ps = ps_t.tile([P, 4, P], F32, name="s_ps", tag="t")
-        nc.tensor.transpose(s_ps[:, 0, :], s_rows[:].bitcast(F32), ident[:])
-        s_col = keep.tile([P, 4], BF16, name="s_col")
-        nc.vector.tensor_copy(out=s_col[:], in_=s_ps[:, 0, 0:2].bitcast(BF16))
 
         u_words = u_sb[:].bitcast(F32)
         v_words = v_sb[:].bitcast(F32)
@@ -89,18 +90,20 @@ def tile_hybridsuperlayer_pa_t_kernel(tc, x, c_fc_U, c_fc_S, c_fc_V, c_fc_bias, 
         u_scales = keep.tile([P, 8 * P], U8, name="u_scales", align_bytes=64)
         v_codes = keep.tile([P, DFF], U32, name="v_codes", align_bytes=64)
         v_scales = keep.tile([P, DFF], U8, name="v_scales", align_bytes=64)
+        s_col = keep.tile([P, 4], BF16, name="s_col")
 
-        def u_bank(b):
+        def u_bank(b, engine):
             tp = ps_t.tile([P, 4, P], F32, name="tp_u", tag="t")
-            for mm in range(2):
-                m = 2 * b + mm
+            for e in range(2):
                 for u in range(2):
-                    lo = (m % 2) * 256 + u * P
-                    nc.tensor.transpose(tp[:, 2 * mm + u, :], u_words[:, m // 2, lo : lo + P], ident[:])
-            nc.scalar.copy(
-                out=g_u_words[:, 2 * b : 2 * b + 2],
-                in_=tp[:].rearrange("p (m u) d -> p m d u", u=2),
-            )
+                    lo = e * 256 + u * P
+                    nc.tensor.transpose(tp[:, 2 * e + u, :], u_words[:, b, lo : lo + P], ident[:])
+            copy_on(engine, g_u_words[:, 2 * b : 2 * b + 2], tp[:].rearrange("p (m u) d -> p m d u", u=2))
+
+        def s_column():
+            s_ps = ps_t.tile([P, 4, P], F32, name="s_ps", tag="t")
+            nc.tensor.transpose(s_ps[:, 0, :], s_rows[:].bitcast(F32), ident[:])
+            nc.vector.tensor_copy(out=s_col[:], in_=s_ps[:, 0, 0:2].bitcast(BF16))
 
         def u_half(g):
             half = g_u[:, 2048 * g : 2048 * (g + 1)]
@@ -128,14 +131,20 @@ def tile_hybridsuperlayer_pa_t_kernel(tc, x, c_fc_U, c_fc_S, c_fc_V, c_fc_bias, 
                 in_=tp[:].rearrange("p (c u) f -> p c f u", u=2),
             )
 
-        u_bank(0)
-        u_bank(1)
+        if WARM:
+            idle_ps = ps_a.tile([P, P], F32, name="idle_ps", tag="a")
+            for k in range(WARM):
+                nc.tensor.matmul(out=idle_ps[:], lhsT=ones[:], rhs=ones[:], start=True, stop=True)
+
+        u_bank(0, "S")
+        u_bank(1, "V")
+        s_column()
         v_bank(0)
         v_bank(1)
         u_half(0)
         nc.vector.quantize_mx(out=v_codes[:].bitcast(FP8X4), scales=v_scales[:], in_=g_v[:])
-        u_bank(2)
-        u_bank(3)
+        u_bank(2, "S")
+        u_bank(3, "S")
         u_half(1)
 
         b_ps = ps_a.tile([P, DFF], F32, name="b_ps", tag="a")
@@ -146,33 +155,39 @@ def tile_hybridsuperlayer_pa_t_kernel(tc, x, c_fc_U, c_fc_S, c_fc_V, c_fc_bias, 
         grouped = {}
         codes = {}
 
-        def flip(n):
+        def flip(n, j, engine):
+            if j == 0:
+                g_x = xgr.tile([P, J * D], BF16, name="g_x", tag="g_x", align_bytes=64)
+                grouped[n] = g_x
             words = x_tiles[n][:].bitcast(F32)
-            g_x = xgr.tile([P, J * D], BF16, name="g_x", tag="g_x", align_bytes=64)
-            g_x_words = g_x[:].bitcast(F32).rearrange("p (j g t u) -> p j g t u", j=J, g=2, t=P, u=2)
-            for j in range(J):
-                tp = ps_t.tile([P, 4, P], F32, name="tp_x", tag="t")
-                for q in range(4):
-                    lo = j * 512 + q * P
-                    nc.tensor.transpose(tp[:, q, :], words[:, lo : lo + P], ident[:])
-                src = tp[:].rearrange("p (g u) t -> p g t u", u=2)
-                if j == J - 1:
-                    nc.vector.tensor_copy(out=g_x_words[:, j], in_=src)
-                else:
-                    nc.scalar.copy(out=g_x_words[:, j], in_=src)
-            grouped[n] = g_x
+            g_x_words = (
+                grouped[n][:].bitcast(F32).rearrange("p (j g t u) -> p j g t u", j=J, g=2, t=P, u=2)
+            )
+            tp = ps_t.tile([P, 4, P], F32, name="tp_x", tag="t")
+            for q in range(4):
+                lo = j * 512 + q * P
+                nc.tensor.transpose(tp[:, q, :], words[:, lo : lo + P], ident[:])
+            copy_on(engine, g_x_words[:, j], tp[:].rearrange("p (g u) t -> p g t u", u=2))
+            if j == J - 1 and n + XBUFS < NG:
+                load(n + XBUFS)
 
-        def quantise(n):
-            x_codes = xq.tile([P, J * 256], U32, name="x_codes", tag="x_codes", align_bytes=64)
-            x_scales = xq.tile([P, J * 256], U8, name="x_scales", tag="x_scales", align_bytes=64)
-            nc.vector.quantize_mx(out=x_codes[:].bitcast(FP8X4), scales=x_scales[:], in_=grouped[n][:])
-            codes[n] = (x_codes, x_scales)
+        def quantise(n, first, count):
+            if first == 0:
+                x_codes = xq.tile([P, J * 256], U32, name="x_codes", tag="x_codes", align_bytes=64)
+                x_scales = xq.tile([P, J * 256], U8, name="x_scales", tag="x_scales", align_bytes=64)
+                codes[n] = (x_codes, x_scales)
+            x_codes, x_scales = codes[n]
+            nc.vector.quantize_mx(
+                out=x_codes[:, first * 256 : (first + count) * 256].bitcast(FP8X4),
+                scales=x_scales[:, first * 256 : (first + count) * 256],
+                in_=grouped[n][:, first * D : (first + count) * D],
+            )
 
         g_w = keep.tile([P, 2, DFF, 4], BF16, name="g_w", align_bytes=64)
         w_codes = keep.tile([P, 2, DFF], U32, name="w_codes", align_bytes=64)
         w_scales = keep.tile([P, 2, DFF], U8, name="w_scales", align_bytes=64)
 
-        def w_half(g):
+        def w_half(g, engines):
             for c in range(4):
                 wa = ps_a.tile([P, 4, P], F32, name="wa", tag="a")
                 for t in range(4):
@@ -186,23 +201,21 @@ def tile_hybridsuperlayer_pa_t_kernel(tc, x, c_fc_U, c_fc_S, c_fc_V, c_fc_bias, 
                         start=True,
                         stop=True,
                     )
-                dst = g_w[:, g, c * P : (c + 1) * P, :]
-                src = wa[:].rearrange("p t f -> p f t")
-                if c % 2 == 0:
-                    nc.scalar.copy(out=dst, in_=src)
-                else:
-                    nc.vector.tensor_copy(out=dst, in_=src)
+                copy_on(engines[c], g_w[:, g, c * P : (c + 1) * P, :], wa[:].rearrange("p t f -> p f t"))
             nc.vector.quantize_mx(
                 out=w_codes[:, g, :].bitcast(FP8X4),
                 scales=w_scales[:, g, :],
                 in_=g_w[:, g].rearrange("p f t -> p (f t)"),
             )
 
-        w_half(0)
-        flip(0)
-        load(XBUFS)
-        w_half(1)
-        quantise(0)
+        w_half(0, "SSSV")
+        flip(0, 0, "S")
+        w_half(1, "SVSV")
+        flip(0, 1, "S")
+        quantise(0, 0, 2)
+        flip(0, 2, "S")
+        flip(0, 3, "S")
+        quantise(0, 2, 2)
 
         waiting = []
 
@@ -229,20 +242,19 @@ def tile_hybridsuperlayer_pa_t_kernel(tc, x, c_fc_U, c_fc_S, c_fc_V, c_fc_bias, 
             n, o_sb, j = waiting[i]
             cols = o_sb[:, j * DFF : (j + 1) * DFF]
             nc.scalar.activation(out=cols, in_=cols, func=GELU)
-            if n == NG - 1:
+            if n >= NG - FINE_STORES:
                 nc.sync.dma_start(out=out_groups[n][:, j * DFF : (j + 1) * DFF], in_=cols)
             elif j == J - 1:
                 nc.sync.dma_start(out=out_groups[n], in_=o_sb[:])
 
         for n in range(NG):
             if n + 1 < NG:
-                flip(n + 1)
-            if n + 1 + XBUFS < NG:
-                load(n + 1 + XBUFS)
+                for j in range(J):
+                    flip(n + 1, j, "V" if (j == J - 1 and n > 0) else "S")
             o_sb = res.tile([P, J * DFF], F32, name="o_sb", tag="o_sb")
             for j in range(J):
                 if j == 2 and n + 1 < NG:
-                    quantise(n + 1)
+                    quantise(n + 1, 0, J)
                 product(n, o_sb, j)
                 if n * J + j >= LAG:
                     finish(n * J + j - LAG)

@@ -233,24 +233,33 @@ def tile_hybridsuperlayer_pa_t_kernel(tc, x, c_fc_U, c_fc_S, c_fc_V, c_fc_bias, 
                     start=(g == 0),
                     stop=(g == 1),
                 )
-            nc.vector.tensor_tensor(
-                out=o_sb[:, j * DFF : (j + 1) * DFF], in0=acc[:], in1=bias_bc[:], op=ADD
-            )
-            waiting.append((n, o_sb, j))
+            pieces = 2 if (n == NG - 1 and j == J - 1) else 1
+            width = DFF // pieces
+            for h in range(pieces):
+                nc.vector.tensor_tensor(
+                    out=o_sb[:, j * DFF + h * width : j * DFF + (h + 1) * width],
+                    in0=acc[:, h * width : (h + 1) * width],
+                    in1=bias_bc[:, h * width : (h + 1) * width],
+                    op=ADD,
+                )
+            waiting.append((n, o_sb, j, pieces))
 
         def finish(i):
-            n, o_sb, j = waiting[i]
-            cols = o_sb[:, j * DFF : (j + 1) * DFF]
-            nc.scalar.activation(out=cols, in_=cols, func=GELU)
-            if n >= NG - FINE_STORES:
-                nc.sync.dma_start(out=out_groups[n][:, j * DFF : (j + 1) * DFF], in_=cols)
-            elif j == J - 1:
+            n, o_sb, j, pieces = waiting[i]
+            width = DFF // pieces
+            for h in range(pieces):
+                lo = j * DFF + h * width
+                cols = o_sb[:, lo : lo + width]
+                nc.scalar.activation(out=cols, in_=cols, func=GELU)
+                if n >= NG - FINE_STORES:
+                    nc.sync.dma_start(out=out_groups[n][:, lo : lo + width], in_=cols)
+            if n < NG - FINE_STORES and j == J - 1:
                 nc.sync.dma_start(out=out_groups[n], in_=o_sb[:])
 
         for n in range(NG):
             if n + 1 < NG:
                 for j in range(J):
-                    flip(n + 1, j, "V" if (j == J - 1 and n > 0) else "S")
+                    flip(n + 1, j, "V" if (j == J - 1 and (n + 1) % 5 != 1) else "S")
             o_sb = res.tile([P, J * DFF], F32, name="o_sb", tag="o_sb")
             for j in range(J):
                 if j == 2 and n + 1 < NG:

@@ -22,7 +22,7 @@ FLOPS = 2 * D * RANK * DFF + 2 * TOKENS * D * DFF
 J = 4
 NG = TOKENS // (P * J)
 XBUFS = 8
-LAG = 2
+LAG = 3
 FINE_STORES = 3
 WARM = 0
 
@@ -262,7 +262,7 @@ def tile_hybridsuperlayer_pa_t_kernel(tc, x, c_fc_U, c_fc_S, c_fc_V, c_fc_bias, 
                     flip(n + 1, j, "V" if (j == J - 1 and (n + 1) % 5 != 1) else "S")
             o_sb = res.tile([P, J * DFF], F32, name="o_sb", tag="o_sb")
             for j in range(J):
-                if j == 2 and n + 1 < NG:
+                if j == 1 and n + 1 < NG:
                     quantise(n + 1, 0, J)
                 product(n, o_sb, j)
                 if n * J + j >= LAG:

@@ -19,253 +19,243 @@ DFF = 512
 RANK = 512
 FLOPS = 2 * D * RANK * DFF + 2 * TOKENS * D * DFF
 
-J = 4
-NG = TOKENS // (P * J)
-XBUFS = 8
-LAG = 3
+TILES = 4
+GROUPS = TOKENS // (P * TILES)
+X_BUFS = 8
+OUT_BUFS = 6
+GELU_LAG = 3
 FINE_STORES = 3
-WARM = 0
 
 
 def tile_hybridsuperlayer_pa_t_kernel(tc, x, c_fc_U, c_fc_S, c_fc_V, c_fc_bias, out):
     nc = tc.nc
-    x_groups = x.flatten_outer_dims().rearrange("(n p j) k -> n p (j k)", p=P, j=J)
-    out_groups = out.flatten_outer_dims().rearrange("(n p j) f -> n p (j f)", p=P, j=J)
+    x_groups = x.flatten_outer_dims().rearrange("(n p j) k -> n p (j k)", p=P, j=TILES)
+    out_groups = out.flatten_outer_dims().rearrange("(n p j) f -> n p (j f)", p=P, j=TILES)
+    by_scalar = nc.scalar.copy
+    by_vector = nc.vector.tensor_copy
 
     with ExitStack() as ctx:
         ctx.enter_context(tc.manual_schedule())
         keep = ctx.enter_context(tc.tile_pool(name="keep", bufs=1))
-        xin = ctx.enter_context(tc.tile_pool(name="xin", bufs=XBUFS))
-        xgr = ctx.enter_context(tc.tile_pool(name="xgr", bufs=3))
-        xq = ctx.enter_context(tc.tile_pool(name="xq", bufs=4))
-        res = ctx.enter_context(tc.tile_pool(name="res", bufs=6))
-        ps_t = ctx.enter_context(tc.psum_pool(name="ps_t", bufs=4))
-        ps_a = ctx.enter_context(tc.psum_pool(name="ps_a", bufs=4))
-
-        def copy_on(engine, dst, src):
-            if engine == "V":
-                nc.vector.tensor_copy(out=dst, in_=src)
-            else:
-                nc.scalar.copy(out=dst, in_=src)
+        x_pool = ctx.enter_context(tc.tile_pool(name="x_pool", bufs=X_BUFS))
+        lined_pool = ctx.enter_context(tc.tile_pool(name="lined_pool", bufs=2))
+        mx_pool = ctx.enter_context(tc.tile_pool(name="mx_pool", bufs=2))
+        out_pool = ctx.enter_context(tc.tile_pool(name="out_pool", bufs=OUT_BUFS))
+        flip_banks = ctx.enter_context(tc.psum_pool(name="flip_banks", bufs=4))
+        sum_banks = ctx.enter_context(tc.psum_pool(name="sum_banks", bufs=4))
 
         u_sb = keep.tile([P, 4, 2 * RANK], BF16, name="u_sb")
         v_sb = keep.tile([P, 4, RANK], BF16, name="v_sb")
-        u_view = c_fc_U.rearrange("(c p e) r -> p c (e r)", c=4, p=P, e=2)
-        nc.sync.dma_start(out=u_sb[:, 0:1, :], in_=u_view[:, 0:1, :])
-        nc.sync.dma_start(out=u_sb[:, 1:2, :], in_=u_view[:, 1:2, :])
+        u_rows = c_fc_U.rearrange("(c p e) r -> p c (e r)", c=4, p=P, e=2)
+        nc.sync.dma_start(out=u_sb[:, 0:1, :], in_=u_rows[:, 0:1, :])
+        nc.sync.dma_start(out=u_sb[:, 1:2, :], in_=u_rows[:, 1:2, :])
         nc.sync.dma_start(out=v_sb[:], in_=c_fc_V.rearrange("(c p) r -> p c r", p=P))
-        nc.sync.dma_start(out=u_sb[:, 2:4, :], in_=u_view[:, 2:4, :])
+        nc.sync.dma_start(out=u_sb[:, 2:4, :], in_=u_rows[:, 2:4, :])
 
         x_tiles = {}
 
         def load(n):
-            x_sb = xin.tile([P, J * D], BF16, name="x_sb", tag="x_sb")
+            x_sb = x_pool.tile([P, TILES * D], BF16, name="x_sb")
             nc.sync.dma_start(out=x_sb[:], in_=x_groups[n])
             x_tiles[n] = x_sb
 
-        for n in range(XBUFS):
+        for n in range(X_BUFS):
             load(n)
 
         s_rows = keep.tile([P, 256], BF16, name="s_rows")
         b_rows = keep.tile([P, DFF], BF16, name="b_rows")
         ones = keep.tile([P, P], BF16, name="ones")
-        warm = keep.tile([P, 8], F32, name="warm")
+        scratch = keep.tile([P, 8], F32, name="scratch")
         ident = keep.tile([P, P], F32, name="ident")
         nc.vector.memset(s_rows[:], 0.0)
         nc.vector.memset(b_rows[:], 0.0)
         nc.vector.memset(ones[:], 1.0)
-        nc.vector.memset(warm[:], 0.0)
+        nc.vector.memset(scratch[:], 0.0)
         make_identity(nc, ident[:])
-        nc.scalar.dma_start(out=s_rows[0:2, :], in_=c_fc_S.rearrange("(u w) -> u w", u=2))
+        nc.scalar.dma_start(out=s_rows[0:2, :], in_=c_fc_S.rearrange("(h w) -> h w", h=2))
         nc.scalar.dma_start(out=b_rows[0:1, :], in_=c_fc_bias.rearrange("(o f) -> o f", o=1))
-        nc.scalar.activation(out=warm[:], in_=warm[:], func=GELU)
+        nc.scalar.activation(out=scratch[:], in_=scratch[:], func=GELU)
 
-        u_words = u_sb[:].bitcast(F32)
-        v_words = v_sb[:].bitcast(F32)
-        g_u = keep.tile([P, 8 * 512], BF16, name="g_u", align_bytes=64)
-        g_v = keep.tile([P, 4 * 512], BF16, name="g_v", align_bytes=64)
-        g_u_words = g_u[:].bitcast(F32).rearrange("p (m d u) -> p m d u", m=8, d=P, u=2)
-        g_v_words = g_v[:].bitcast(F32).rearrange("p (c f u) -> p c f u", c=4, f=P, u=2)
-        u_codes = keep.tile([P, 8 * P], U32, name="u_codes", align_bytes=64)
-        u_scales = keep.tile([P, 8 * P], U8, name="u_scales", align_bytes=64)
+        u_pairs = u_sb[:].bitcast(F32)
+        v_pairs = v_sb[:].bitcast(F32)
+        us_lined = keep.tile([P, 8 * 512], BF16, name="us_lined", align_bytes=64)
+        v_lined = keep.tile([P, 4 * 512], BF16, name="v_lined", align_bytes=64)
+        us_lined_pairs = us_lined[:].bitcast(F32).rearrange("p (m d h) -> p m d h", m=8, d=P, h=2)
+        v_lined_pairs = v_lined[:].bitcast(F32).rearrange("p (c f h) -> p c f h", c=4, f=P, h=2)
+        us_codes = keep.tile([P, 8 * P], U32, name="us_codes", align_bytes=64)
+        us_scales = keep.tile([P, 8 * P], U8, name="us_scales", align_bytes=64)
         v_codes = keep.tile([P, DFF], U32, name="v_codes", align_bytes=64)
         v_scales = keep.tile([P, DFF], U8, name="v_scales", align_bytes=64)
         s_col = keep.tile([P, 4], BF16, name="s_col")
 
-        def u_bank(b, engine):
-            tp = ps_t.tile([P, 4, P], F32, name="tp_u", tag="t")
+        def flip_u(c, copy):
+            bank = flip_banks.tile([P, 4, P], F32, name="u_bank", tag="flip")
             for e in range(2):
-                for u in range(2):
-                    lo = e * 256 + u * P
-                    nc.tensor.transpose(tp[:, 2 * e + u, :], u_words[:, b, lo : lo + P], ident[:])
-            copy_on(engine, g_u_words[:, 2 * b : 2 * b + 2], tp[:].rearrange("p (m u) d -> p m d u", u=2))
+                for h in range(2):
+                    lo = 256 * e + P * h
+                    nc.tensor.transpose(bank[:, 2 * e + h, :], u_pairs[:, c, lo : lo + P], ident[:])
+            copy(
+                out=us_lined_pairs[:, 2 * c : 2 * c + 2],
+                in_=bank[:].rearrange("p (e h) d -> p e d h", h=2),
+            )
 
-        def s_column():
-            s_ps = ps_t.tile([P, 4, P], F32, name="s_ps", tag="t")
-            nc.tensor.transpose(s_ps[:, 0, :], s_rows[:].bitcast(F32), ident[:])
-            nc.vector.tensor_copy(out=s_col[:], in_=s_ps[:, 0, 0:2].bitcast(BF16))
+        def flip_s():
+            bank = flip_banks.tile([P, 4, P], F32, name="s_bank", tag="flip")
+            nc.tensor.transpose(bank[:, 0, :], s_rows[:].bitcast(F32), ident[:])
+            nc.vector.tensor_copy(out=s_col[:], in_=bank[:, 0, 0:2].bitcast(BF16))
 
-        def u_half(g):
-            half = g_u[:, 2048 * g : 2048 * (g + 1)]
+        def scale_and_quantise_u(g):
+            lined = us_lined[:, 2048 * g : 2048 * (g + 1)]
             nc.vector.tensor_tensor(
-                out=half.rearrange("p (c t) -> p c t", t=4),
-                in0=half.rearrange("p (c t) -> p c t", t=4),
+                out=lined.rearrange("p (c t) -> p c t", t=4),
+                in0=lined.rearrange("p (c t) -> p c t", t=4),
                 in1=s_col[:].unsqueeze(1).to_broadcast([P, 512, 4]),
                 op=MULT,
             )
             nc.vector.quantize_mx(
-                out=u_codes[:, 512 * g : 512 * (g + 1)].bitcast(FP8X4),
-                scales=u_scales[:, 512 * g : 512 * (g + 1)],
-                in_=half,
+                out=us_codes[:, 512 * g : 512 * (g + 1)].bitcast(FP8X4),
+                scales=us_scales[:, 512 * g : 512 * (g + 1)],
+                in_=lined,
             )
 
-        def v_bank(b):
-            tp = ps_t.tile([P, 4, P], F32, name="tp_v", tag="t")
-            for cc in range(2):
-                for u in range(2):
+        def flip_v(b):
+            bank = flip_banks.tile([P, 4, P], F32, name="v_bank", tag="flip")
+            for c in range(2):
+                for h in range(2):
                     nc.tensor.transpose(
-                        tp[:, 2 * cc + u, :], v_words[:, 2 * b + cc, u * P : (u + 1) * P], ident[:]
+                        bank[:, 2 * c + h, :], v_pairs[:, 2 * b + c, P * h : P * (h + 1)], ident[:]
                     )
             nc.scalar.copy(
-                out=g_v_words[:, 2 * b : 2 * b + 2],
-                in_=tp[:].rearrange("p (c u) f -> p c f u", u=2),
+                out=v_lined_pairs[:, 2 * b : 2 * b + 2],
+                in_=bank[:].rearrange("p (c h) f -> p c f h", h=2),
             )
 
-        if WARM:
-            idle_ps = ps_a.tile([P, P], F32, name="idle_ps", tag="a")
-            for k in range(WARM):
-                nc.tensor.matmul(out=idle_ps[:], lhsT=ones[:], rhs=ones[:], start=True, stop=True)
+        x_lined = {}
+        x_mx = {}
 
-        u_bank(0, "S")
-        u_bank(1, "V")
-        s_column()
-        v_bank(0)
-        v_bank(1)
-        u_half(0)
-        nc.vector.quantize_mx(out=v_codes[:].bitcast(FP8X4), scales=v_scales[:], in_=g_v[:])
-        u_bank(2, "S")
-        u_bank(3, "S")
-        u_half(1)
-
-        b_ps = ps_a.tile([P, DFF], F32, name="b_ps", tag="a")
-        nc.tensor.matmul(out=b_ps[:], lhsT=ones[:], rhs=b_rows[:], start=True, stop=True)
-        bias_bc = keep.tile([P, DFF], F32, name="bias_bc")
-        nc.scalar.copy(out=bias_bc[:], in_=b_ps[:])
-
-        grouped = {}
-        codes = {}
-
-        def flip(n, j, engine):
+        def flip_x(n, j, copy):
             if j == 0:
-                g_x = xgr.tile([P, J * D], BF16, name="g_x", tag="g_x", align_bytes=64)
-                grouped[n] = g_x
-            words = x_tiles[n][:].bitcast(F32)
-            g_x_words = (
-                grouped[n][:].bitcast(F32).rearrange("p (j g t u) -> p j g t u", j=J, g=2, t=P, u=2)
+                lined = lined_pool.tile([P, TILES * D], BF16, name="lined", align_bytes=64)
+                x_lined[n] = lined
+            pairs = x_tiles[n][:].bitcast(F32)
+            lined_pairs = (
+                x_lined[n][:]
+                .bitcast(F32)
+                .rearrange("p (j g t h) -> p j g t h", j=TILES, g=2, t=P, h=2)
             )
-            tp = ps_t.tile([P, 4, P], F32, name="tp_x", tag="t")
+            bank = flip_banks.tile([P, 4, P], F32, name="x_bank", tag="flip")
             for q in range(4):
-                lo = j * 512 + q * P
-                nc.tensor.transpose(tp[:, q, :], words[:, lo : lo + P], ident[:])
-            copy_on(engine, g_x_words[:, j], tp[:].rearrange("p (g u) t -> p g t u", u=2))
-            if j == J - 1 and n + XBUFS < NG:
-                load(n + XBUFS)
+                lo = 512 * j + P * q
+                nc.tensor.transpose(bank[:, q, :], pairs[:, lo : lo + P], ident[:])
+            copy(out=lined_pairs[:, j], in_=bank[:].rearrange("p (g h) t -> p g t h", h=2))
 
-        def quantise(n, first, count):
+        def quantise_x(n, first, count):
             if first == 0:
-                x_codes = xq.tile([P, J * 256], U32, name="x_codes", tag="x_codes", align_bytes=64)
-                x_scales = xq.tile([P, J * 256], U8, name="x_scales", tag="x_scales", align_bytes=64)
-                codes[n] = (x_codes, x_scales)
-            x_codes, x_scales = codes[n]
+                codes = mx_pool.tile([P, TILES * 256], U32, name="codes", align_bytes=64)
+                scales = mx_pool.tile([P, TILES * 256], U8, name="scales", align_bytes=64)
+                x_mx[n] = (codes, scales)
+            codes, scales = x_mx[n]
             nc.vector.quantize_mx(
-                out=x_codes[:, first * 256 : (first + count) * 256].bitcast(FP8X4),
-                scales=x_scales[:, first * 256 : (first + count) * 256],
-                in_=grouped[n][:, first * D : (first + count) * D],
+                out=codes[:, 256 * first : 256 * (first + count)].bitcast(FP8X4),
+                scales=scales[:, 256 * first : 256 * (first + count)],
+                in_=x_lined[n][:, D * first : D * (first + count)],
             )
 
-        g_w = keep.tile([P, 2, DFF, 4], BF16, name="g_w", align_bytes=64)
+        w_lined = keep.tile([P, 2, DFF, 4], BF16, name="w_lined", align_bytes=64)
         w_codes = keep.tile([P, 2, DFF], U32, name="w_codes", align_bytes=64)
         w_scales = keep.tile([P, 2, DFF], U8, name="w_scales", align_bytes=64)
 
-        def w_half(g, engines):
+        def make_w(g, copies):
             for c in range(4):
-                wa = ps_a.tile([P, 4, P], F32, name="wa", tag="a")
+                bank = sum_banks.tile([P, 4, P], F32, name="w_bank", tag="sum")
                 for t in range(4):
-                    lo = (4 * g + t) * P
+                    lo = P * (4 * g + t)
                     nc.tensor.matmul_mx(
-                        out=wa[:, t, :],
-                        lhsT=u_codes[:, lo : lo + P].bitcast(FP8X4),
-                        lhsT_scale=u_scales[:, lo : lo + P],
-                        rhs=v_codes[:, c * P : (c + 1) * P].bitcast(FP8X4),
-                        rhs_scale=v_scales[:, c * P : (c + 1) * P],
+                        out=bank[:, t, :],
+                        lhsT=us_codes[:, lo : lo + P].bitcast(FP8X4),
+                        lhsT_scale=us_scales[:, lo : lo + P],
+                        rhs=v_codes[:, P * c : P * (c + 1)].bitcast(FP8X4),
+                        rhs_scale=v_scales[:, P * c : P * (c + 1)],
                         start=True,
                         stop=True,
                     )
-                copy_on(engines[c], g_w[:, g, c * P : (c + 1) * P, :], wa[:].rearrange("p t f -> p f t"))
+                copy = copies[c]
+                copy(out=w_lined[:, g, P * c : P * (c + 1), :], in_=bank[:].rearrange("p t f -> p f t"))
             nc.vector.quantize_mx(
                 out=w_codes[:, g, :].bitcast(FP8X4),
                 scales=w_scales[:, g, :],
-                in_=g_w[:, g].rearrange("p f t -> p (f t)"),
+                in_=w_lined[:, g].rearrange("p f t -> p (f t)"),
             )
 
-        w_half(0, "SSSV")
-        flip(0, 0, "S")
-        w_half(1, "SVSV")
-        flip(0, 1, "S")
-        quantise(0, 0, 2)
-        flip(0, 2, "S")
-        flip(0, 3, "S")
-        quantise(0, 2, 2)
+        flip_u(0, by_scalar)
+        flip_u(1, by_vector)
+        flip_s()
+        flip_v(0)
+        flip_v(1)
+        scale_and_quantise_u(0)
+        nc.vector.quantize_mx(out=v_codes[:].bitcast(FP8X4), scales=v_scales[:], in_=v_lined[:])
+        flip_u(2, by_scalar)
+        flip_u(3, by_scalar)
+        scale_and_quantise_u(1)
 
-        waiting = []
+        bias_bank = sum_banks.tile([P, DFF], F32, name="bias_bank", tag="sum")
+        nc.tensor.matmul(out=bias_bank[:], lhsT=ones[:], rhs=b_rows[:], start=True, stop=True)
+        bias_all = keep.tile([P, DFF], F32, name="bias_all")
+        nc.scalar.copy(out=bias_all[:], in_=bias_bank[:])
 
-        def product(n, o_sb, j):
-            x_codes, x_scales = codes[n]
-            acc = ps_a.tile([P, DFF], F32, name="acc", tag="a")
+        make_w(0, (by_scalar, by_scalar, by_scalar, by_vector))
+        flip_x(0, 0, by_scalar)
+        make_w(1, (by_scalar, by_vector, by_scalar, by_vector))
+        flip_x(0, 1, by_scalar)
+        quantise_x(0, 0, 2)
+        flip_x(0, 2, by_scalar)
+        flip_x(0, 3, by_scalar)
+        load(X_BUFS)
+        quantise_x(0, 2, 2)
+
+        results = {}
+
+        def multiply_and_add_bias(n, j):
+            if j == 0:
+                o_sb = out_pool.tile([P, TILES * DFF], F32, name="o_sb")
+                results[n] = o_sb
+            codes, scales = x_mx[n]
+            bank = sum_banks.tile([P, DFF], F32, name="h_bank", tag="sum")
             for g in range(2):
-                lo = (2 * j + g) * P
+                lo = P * (2 * j + g)
                 nc.tensor.matmul_mx(
-                    out=acc[:],
-                    lhsT=x_codes[:, lo : lo + P].bitcast(FP8X4),
-                    lhsT_scale=x_scales[:, lo : lo + P],
+                    out=bank[:],
+                    lhsT=codes[:, lo : lo + P].bitcast(FP8X4),
+                    lhsT_scale=scales[:, lo : lo + P],
                     rhs=w_codes[:, g, :].bitcast(FP8X4),
                     rhs_scale=w_scales[:, g, :],
                     start=(g == 0),
                     stop=(g == 1),
                 )
-            pieces = 2 if (n == NG - 1 and j == J - 1) else 1
-            width = DFF // pieces
-            for h in range(pieces):
-                nc.vector.tensor_tensor(
-                    out=o_sb[:, j * DFF + h * width : j * DFF + (h + 1) * width],
-                    in0=acc[:, h * width : (h + 1) * width],
-                    in1=bias_bc[:, h * width : (h + 1) * width],
-                    op=ADD,
-                )
-            waiting.append((n, o_sb, j, pieces))
+            nc.vector.tensor_tensor(
+                out=results[n][:, DFF * j : DFF * (j + 1)], in0=bank[:], in1=bias_all[:], op=ADD
+            )
 
-        def finish(i):
-            n, o_sb, j, pieces = waiting[i]
-            width = DFF // pieces
-            for h in range(pieces):
-                lo = j * DFF + h * width
-                cols = o_sb[:, lo : lo + width]
-                nc.scalar.activation(out=cols, in_=cols, func=GELU)
-                if n >= NG - FINE_STORES:
-                    nc.sync.dma_start(out=out_groups[n][:, lo : lo + width], in_=cols)
-            if n < NG - FINE_STORES and j == J - 1:
-                nc.sync.dma_start(out=out_groups[n], in_=o_sb[:])
+        def gelu_and_store(n, j):
+            cols = results[n][:, DFF * j : DFF * (j + 1)]
+            nc.scalar.activation(out=cols, in_=cols, func=GELU)
+            if n >= GROUPS - FINE_STORES:
+                nc.sync.dma_start(out=out_groups[n][:, DFF * j : DFF * (j + 1)], in_=cols)
+            elif j == TILES - 1:
+                nc.sync.dma_start(out=out_groups[n], in_=results[n][:])
 
-        for n in range(NG):
-            if n + 1 < NG:
-                for j in range(J):
-                    flip(n + 1, j, "V" if (j == J - 1 and (n + 1) % 5 != 1) else "S")
-            o_sb = res.tile([P, J * DFF], F32, name="o_sb", tag="o_sb")
-            for j in range(J):
-                if j == 1 and n + 1 < NG:
-                    quantise(n + 1, 0, J)
-                product(n, o_sb, j)
-                if n * J + j >= LAG:
-                    finish(n * J + j - LAG)
-        for i in range(NG * J - LAG, NG * J):
-            finish(i)
+        for n in range(GROUPS):
+            if n + 1 < GROUPS:
+                for j in range(TILES):
+                    flip_x(n + 1, j, by_vector if (j == TILES - 1 and n > 0) else by_scalar)
+            if n + 1 + X_BUFS < GROUPS:
+                load(n + 1 + X_BUFS)
+            for j in range(TILES):
+                if j == 1 and n + 1 < GROUPS:
+                    quantise_x(n + 1, 0, TILES)
+                multiply_and_add_bias(n, j)
+                done = TILES * n + j - GELU_LAG
+                if done >= 0:
+                    gelu_and_store(done // TILES, done % TILES)
+        for done in range(TILES * GROUPS - GELU_LAG, TILES * GROUPS):
+            gelu_and_store(done // TILES, done % TILES)

from contextlib import ExitStack

import concourse.mybir as mybir
from concourse.masks import make_identity

F32 = mybir.dt.float32
BF16 = mybir.dt.bfloat16
U32 = mybir.dt.uint32
U8 = mybir.dt.uint8
FP8X4 = mybir.dt.float8_e4m3fn_x4
GELU = mybir.ActivationFunctionType.Gelu
MULT = mybir.AluOpType.mult
ADD = mybir.AluOpType.add

P = 128
TOKENS = 8192
D = 1024
DFF = 512
RANK = 512
FLOPS = 2 * D * RANK * DFF + 2 * TOKENS * D * DFF

TILES = 4
GROUPS = TOKENS // (P * TILES)
X_BUFS = 8
OUT_BUFS = 6
GELU_LAG = 3
FINE_STORES = 3


def tile_hybridsuperlayer_pa_t_kernel(tc, x, c_fc_U, c_fc_S, c_fc_V, c_fc_bias, out):
    nc = tc.nc
    x_groups = x.flatten_outer_dims().rearrange("(n p j) k -> n p (j k)", p=P, j=TILES)
    out_groups = out.flatten_outer_dims().rearrange("(n p j) f -> n p (j f)", p=P, j=TILES)
    by_scalar = nc.scalar.copy
    by_vector = nc.vector.tensor_copy

    with ExitStack() as ctx:
        ctx.enter_context(tc.manual_schedule())
        keep = ctx.enter_context(tc.tile_pool(name="keep", bufs=1))
        x_pool = ctx.enter_context(tc.tile_pool(name="x_pool", bufs=X_BUFS))
        lined_pool = ctx.enter_context(tc.tile_pool(name="lined_pool", bufs=2))
        mx_pool = ctx.enter_context(tc.tile_pool(name="mx_pool", bufs=2))
        out_pool = ctx.enter_context(tc.tile_pool(name="out_pool", bufs=OUT_BUFS))
        flip_banks = ctx.enter_context(tc.psum_pool(name="flip_banks", bufs=4))
        sum_banks = ctx.enter_context(tc.psum_pool(name="sum_banks", bufs=4))

        u_sb = keep.tile([P, 4, 2 * RANK], BF16, name="u_sb")
        v_sb = keep.tile([P, 4, RANK], BF16, name="v_sb")
        u_rows = c_fc_U.rearrange("(c p e) r -> p c (e r)", c=4, p=P, e=2)
        nc.sync.dma_start(out=u_sb[:, 0:1, :], in_=u_rows[:, 0:1, :])
        nc.sync.dma_start(out=u_sb[:, 1:2, :], in_=u_rows[:, 1:2, :])
        nc.sync.dma_start(out=v_sb[:], in_=c_fc_V.rearrange("(c p) r -> p c r", p=P))
        nc.sync.dma_start(out=u_sb[:, 2:4, :], in_=u_rows[:, 2:4, :])

        x_tiles = {}

        def load(n):
            x_sb = x_pool.tile([P, TILES * D], BF16, name="x_sb")
            nc.sync.dma_start(out=x_sb[:], in_=x_groups[n])
            x_tiles[n] = x_sb

        for n in range(X_BUFS):
            load(n)

        s_rows = keep.tile([P, 256], BF16, name="s_rows")
        b_rows = keep.tile([P, DFF], BF16, name="b_rows")
        ones = keep.tile([P, P], BF16, name="ones")
        scratch = keep.tile([P, 8], F32, name="scratch")
        ident = keep.tile([P, P], F32, name="ident")
        nc.vector.memset(s_rows[:], 0.0)
        nc.vector.memset(b_rows[:], 0.0)
        nc.vector.memset(ones[:], 1.0)
        nc.vector.memset(scratch[:], 0.0)
        make_identity(nc, ident[:])
        nc.scalar.dma_start(out=s_rows[0:2, :], in_=c_fc_S.rearrange("(h w) -> h w", h=2))
        nc.scalar.dma_start(out=b_rows[0:1, :], in_=c_fc_bias.rearrange("(o f) -> o f", o=1))
        nc.scalar.activation(out=scratch[:], in_=scratch[:], func=GELU)

        u_pairs = u_sb[:].bitcast(F32)
        v_pairs = v_sb[:].bitcast(F32)
        us_lined = keep.tile([P, 8 * 512], BF16, name="us_lined", align_bytes=64)
        v_lined = keep.tile([P, 4 * 512], BF16, name="v_lined", align_bytes=64)
        us_lined_pairs = us_lined[:].bitcast(F32).rearrange("p (m d h) -> p m d h", m=8, d=P, h=2)
        v_lined_pairs = v_lined[:].bitcast(F32).rearrange("p (c f h) -> p c f h", c=4, f=P, h=2)
        us_codes = keep.tile([P, 8 * P], U32, name="us_codes", align_bytes=64)
        us_scales = keep.tile([P, 8 * P], U8, name="us_scales", align_bytes=64)
        v_codes = keep.tile([P, DFF], U32, name="v_codes", align_bytes=64)
        v_scales = keep.tile([P, DFF], U8, name="v_scales", align_bytes=64)
        s_col = keep.tile([P, 4], BF16, name="s_col")

        def flip_u(c, copy):
            bank = flip_banks.tile([P, 4, P], F32, name="u_bank", tag="flip")
            for e in range(2):
                for h in range(2):
                    lo = 256 * e + P * h
                    nc.tensor.transpose(bank[:, 2 * e + h, :], u_pairs[:, c, lo : lo + P], ident[:])
            copy(
                out=us_lined_pairs[:, 2 * c : 2 * c + 2],
                in_=bank[:].rearrange("p (e h) d -> p e d h", h=2),
            )

        def flip_s():
            bank = flip_banks.tile([P, 4, P], F32, name="s_bank", tag="flip")
            nc.tensor.transpose(bank[:, 0, :], s_rows[:].bitcast(F32), ident[:])
            nc.vector.tensor_copy(out=s_col[:], in_=bank[:, 0, 0:2].bitcast(BF16))

        def scale_and_quantise_u(g):
            lined = us_lined[:, 2048 * g : 2048 * (g + 1)]
            nc.vector.tensor_tensor(
                out=lined.rearrange("p (c t) -> p c t", t=4),
                in0=lined.rearrange("p (c t) -> p c t", t=4),
                in1=s_col[:].unsqueeze(1).to_broadcast([P, 512, 4]),
                op=MULT,
            )
            nc.vector.quantize_mx(
                out=us_codes[:, 512 * g : 512 * (g + 1)].bitcast(FP8X4),
                scales=us_scales[:, 512 * g : 512 * (g + 1)],
                in_=lined,
            )

        def flip_v(b):
            bank = flip_banks.tile([P, 4, P], F32, name="v_bank", tag="flip")
            for c in range(2):
                for h in range(2):
                    nc.tensor.transpose(
                        bank[:, 2 * c + h, :], v_pairs[:, 2 * b + c, P * h : P * (h + 1)], ident[:]
                    )
            nc.scalar.copy(
                out=v_lined_pairs[:, 2 * b : 2 * b + 2],
                in_=bank[:].rearrange("p (c h) f -> p c f h", h=2),
            )

        x_lined = {}
        x_mx = {}

        def flip_x(n, j, copy):
            if j == 0:
                lined = lined_pool.tile([P, TILES * D], BF16, name="lined", align_bytes=64)
                x_lined[n] = lined
            pairs = x_tiles[n][:].bitcast(F32)
            lined_pairs = (
                x_lined[n][:]
                .bitcast(F32)
                .rearrange("p (j g t h) -> p j g t h", j=TILES, g=2, t=P, h=2)
            )
            bank = flip_banks.tile([P, 4, P], F32, name="x_bank", tag="flip")
            for q in range(4):
                lo = 512 * j + P * q
                nc.tensor.transpose(bank[:, q, :], pairs[:, lo : lo + P], ident[:])
            copy(out=lined_pairs[:, j], in_=bank[:].rearrange("p (g h) t -> p g t h", h=2))

        def quantise_x(n, first, count):
            if first == 0:
                codes = mx_pool.tile([P, TILES * 256], U32, name="codes", align_bytes=64)
                scales = mx_pool.tile([P, TILES * 256], U8, name="scales", align_bytes=64)
                x_mx[n] = (codes, scales)
            codes, scales = x_mx[n]
            nc.vector.quantize_mx(
                out=codes[:, 256 * first : 256 * (first + count)].bitcast(FP8X4),
                scales=scales[:, 256 * first : 256 * (first + count)],
                in_=x_lined[n][:, D * first : D * (first + count)],
            )

        w_lined = keep.tile([P, 2, DFF, 4], BF16, name="w_lined", align_bytes=64)
        w_codes = keep.tile([P, 2, DFF], U32, name="w_codes", align_bytes=64)
        w_scales = keep.tile([P, 2, DFF], U8, name="w_scales", align_bytes=64)

        def make_w(g, copies):
            for c in range(4):
                bank = sum_banks.tile([P, 4, P], F32, name="w_bank", tag="sum")
                for t in range(4):
                    lo = P * (4 * g + t)
                    nc.tensor.matmul_mx(
                        out=bank[:, t, :],
                        lhsT=us_codes[:, lo : lo + P].bitcast(FP8X4),
                        lhsT_scale=us_scales[:, lo : lo + P],
                        rhs=v_codes[:, P * c : P * (c + 1)].bitcast(FP8X4),
                        rhs_scale=v_scales[:, P * c : P * (c + 1)],
                        start=True,
                        stop=True,
                    )
                copy = copies[c]
                copy(out=w_lined[:, g, P * c : P * (c + 1), :], in_=bank[:].rearrange("p t f -> p f t"))
            nc.vector.quantize_mx(
                out=w_codes[:, g, :].bitcast(FP8X4),
                scales=w_scales[:, g, :],
                in_=w_lined[:, g].rearrange("p f t -> p (f t)"),
            )

        flip_u(0, by_scalar)
        flip_u(1, by_vector)
        flip_s()
        flip_v(0)
        flip_v(1)
        scale_and_quantise_u(0)
        nc.vector.quantize_mx(out=v_codes[:].bitcast(FP8X4), scales=v_scales[:], in_=v_lined[:])
        flip_u(2, by_scalar)
        flip_u(3, by_scalar)
        scale_and_quantise_u(1)

        bias_bank = sum_banks.tile([P, DFF], F32, name="bias_bank", tag="sum")
        nc.tensor.matmul(out=bias_bank[:], lhsT=ones[:], rhs=b_rows[:], start=True, stop=True)
        bias_all = keep.tile([P, DFF], F32, name="bias_all")
        nc.scalar.copy(out=bias_all[:], in_=bias_bank[:])

        make_w(0, (by_scalar, by_scalar, by_scalar, by_vector))
        flip_x(0, 0, by_scalar)
        make_w(1, (by_scalar, by_vector, by_scalar, by_vector))
        flip_x(0, 1, by_scalar)
        quantise_x(0, 0, 2)
        flip_x(0, 2, by_scalar)
        flip_x(0, 3, by_scalar)
        load(X_BUFS)
        quantise_x(0, 2, 2)

        results = {}

        def multiply_and_add_bias(n, j):
            if j == 0:
                o_sb = out_pool.tile([P, TILES * DFF], F32, name="o_sb")
                results[n] = o_sb
            codes, scales = x_mx[n]
            bank = sum_banks.tile([P, DFF], F32, name="h_bank", tag="sum")
            for g in range(2):
                lo = P * (2 * j + g)
                nc.tensor.matmul_mx(
                    out=bank[:],
                    lhsT=codes[:, lo : lo + P].bitcast(FP8X4),
                    lhsT_scale=scales[:, lo : lo + P],
                    rhs=w_codes[:, g, :].bitcast(FP8X4),
                    rhs_scale=w_scales[:, g, :],
                    start=(g == 0),
                    stop=(g == 1),
                )
            nc.vector.tensor_tensor(
                out=results[n][:, DFF * j : DFF * (j + 1)], in0=bank[:], in1=bias_all[:], op=ADD
            )

        def gelu_and_store(n, j):
            cols = results[n][:, DFF * j : DFF * (j + 1)]
            nc.scalar.activation(out=cols, in_=cols, func=GELU)
            if n >= GROUPS - FINE_STORES:
                nc.sync.dma_start(out=out_groups[n][:, DFF * j : DFF * (j + 1)], in_=cols)
            elif j == TILES - 1:
                nc.sync.dma_start(out=out_groups[n], in_=results[n][:])

        for n in range(GROUPS):
            if n + 1 < GROUPS:
                for j in range(TILES):
                    flip_x(n + 1, j, by_vector if (j == TILES - 1 and n > 0) else by_scalar)
            if n + 1 + X_BUFS < GROUPS:
                load(n + 1 + X_BUFS)
            for j in range(TILES):
                if j == 1 and n + 1 < GROUPS:
                    quantise_x(n + 1, 0, TILES)
                multiply_and_add_bias(n, j)
                done = TILES * n + j - GELU_LAG
                if done >= 0:
                    gelu_and_store(done // TILES, done % TILES)
        for done in range(TILES * GROUPS - GELU_LAG, TILES * GROUPS):
            gelu_and_store(done // TILES, done % TILES)
